import numpy as np
import ml_dtypes


def mxq(x, axis, fmt="e4m3"):
    dtype, down = {"e4m3": (ml_dtypes.float8_e4m3fn, 7), "e5m2": (ml_dtypes.float8_e5m2, 14)}[fmt]
    v = np.moveaxis(np.asarray(x, np.float32).astype(ml_dtypes.bfloat16).astype(np.float64), axis, -1)
    blocks = v.reshape(v.shape[:-1] + (-1, 32))
    amax = np.abs(blocks).max(-1, keepdims=True)
    byte = np.maximum(np.where(amax > 0, np.frexp(amax)[1] - 1 + 127, 0) - down, 1)
    scale = np.exp2(byte - 127.0)
    codes = (blocks / scale).astype(np.float32).astype(dtype).astype(np.float64)
    return np.moveaxis((codes * scale).reshape(v.shape), -1, axis)


WIDE = False


def mx_kscale(k):
    if not WIDE:
        return np.ones(k)
    levels = np.array([10, -10, 5, -5, 0])
    a = np.random.permutation(np.resize(levels, k // 512 * 4)).reshape(k // 512, 4)
    idx = np.arange(k)
    return np.exp2(a[idx // 512, idx % 128 // 32])


BF16 = ml_dtypes.bfloat16


def bf(x):
    return np.asarray(x, np.float32).astype(BF16)


def f64(x):
    return np.asarray(x).astype(np.float64)


B, S, D, N = 128, 64, 1024, 256
EPS = 1e-5


def batch_bn(x, g, b):
    m = x.mean(axis=0)
    v = x.var(axis=0)
    return g * (x - m) / np.sqrt(v + EPS) + b


def setup_inputs():
    t, u = mx_kscale(D), mx_kscale(D)
    return {"s_z2": bf(np.random.standard_normal((B, S, D)) * 0.6 + np.random.standard_normal(D) * 0.4),
            "c_z2": bf(np.random.standard_normal((B, D)) * 0.6 + np.random.standard_normal(D) * 0.4),
            "s_g2": bf((1.0 + 0.1 * np.random.standard_normal(D)) * t),
            "s_be2": bf(0.1 * np.random.standard_normal(D) * t),
            "s_w3": bf(np.random.standard_normal((N, D)) * np.sqrt(2.0 / D) / t[None, :]),
            "s_b3": bf(0.1 * np.random.standard_normal(N)),
            "c_g2": bf((1.0 + 0.1 * np.random.standard_normal(D)) * u),
            "c_be2": bf(0.1 * np.random.standard_normal(D) * u),
            "c_w3": bf(np.random.standard_normal((N, D)) * np.sqrt(2.0 / D) / u[None, :]),
            "c_b3": bf(0.1 * np.random.standard_normal(N))}


def reference(s_z2, c_z2, s_g2, s_be2, s_w3, s_b3, c_g2, c_be2, c_w3, c_b3):
    c_h = np.maximum(batch_bn(f64(c_z2), f64(c_g2), f64(c_be2)), 0.0)
    c_out = (mxq(c_h, 1, "e4m3") @ mxq(f64(c_w3), 1, "e4m3").T) + f64(c_b3)
    s_h = np.maximum(batch_bn(f64(s_z2), f64(s_g2), f64(s_be2)), 0.0)
    s_p = (mxq(s_h, 2, "e4m3") @ mxq(f64(s_w3), 1, "e4m3").T) + f64(s_b3)
    s_out = s_p * c_out[:, None, :]
    aggregated_c = s_out.max(axis=1)
    return (s_out, aggregated_c)

@@ -1,0 +1,358 @@
+from contextlib import ExitStack
+
+import concourse.mybir as mybir
+from concourse.masks import make_identity
+
+BF16 = mybir.dt.bfloat16
+F32 = mybir.dt.float32
+U32 = mybir.dt.uint32
+U8 = mybir.dt.uint8
+FP8X4 = mybir.dt.float8_e4m3fn_x4
+ACT = mybir.ActivationFunctionType
+ALU = mybir.AluOpType
+
+P = 128
+SLICES = 64
+FEATURES = 1024
+OUT = 256
+EPS = 1e-5
+CHUNKS = FEATURES // P
+PACK = 4
+PASSES = FEATURES // (P * PACK)
+GROUP = 2
+JOBS = 1 + SLICES // GROUP
+HALVES = OUT // P
+
+FLOPS = 2 * (SLICES + 1) * P * FEATURES * OUT
+
+
+def tile_cgblock_pb_t_kernel(
+    tc, s_z2, c_z2, s_g2, s_be2, s_w3, s_b3, c_g2, c_be2, c_w3, c_b3, out_0, out_1
+):
+    nc = tc.nc
+    with ExitStack() as stack:
+        stack.enter_context(tc.manual_schedule())
+        const = stack.enter_context(tc.tile_pool(name="const", bufs=1))
+        small = stack.enter_context(tc.tile_pool(name="small", bufs=4))
+        work = stack.enter_context(tc.tile_pool(name="work", bufs=3))
+        results = stack.enter_context(tc.tile_pool(name="results", bufs=6))
+        psum_x = stack.enter_context(tc.psum_pool(name="psum_x", bufs=6))
+        psum_sum = stack.enter_context(tc.psum_pool(name="psum_sum", bufs=1))
+        psum_acc = stack.enter_context(tc.psum_pool(name="psum_acc", bufs=1))
+
+        vec_rows = const.tile([P, P], BF16)
+        nc.vector.memset(vec_rows[:], 0.0)
+        for r, vec in enumerate((s_g2, s_be2, c_g2, c_be2)):
+            nc.scalar.dma_start(
+                out=vec_rows[r * CHUNKS : (r + 1) * CHUNKS, :],
+                in_=vec.rearrange("(c p) -> c p", p=P),
+            )
+        c_w_raw = const.tile([P, HALVES, FEATURES], BF16)
+        nc.sync.dma_start(out=c_w_raw[:], in_=c_w3.rearrange("(h n) k -> n h k", n=P))
+        s_w_raw = const.tile([P, HALVES, FEATURES], BF16)
+        nc.sync.dma_start(out=s_w_raw[:], in_=s_w3.rearrange("(h n) k -> n h k", n=P))
+        c_x = const.tile([P, FEATURES], BF16)
+        nc.sync.dma_start(out=c_x[:], in_=c_z2)
+        c_bias = const.tile([P, OUT], BF16)
+        nc.scalar.dma_start(out=c_bias[:], in_=c_b3.partition_broadcast(P))
+        s_bias = const.tile([P, OUT], BF16)
+        nc.scalar.dma_start(out=s_bias[:], in_=s_b3.partition_broadcast(P))
+        x_tiles = []
+        for first in range(0, SLICES, GROUP):
+            x_tile = const.tile([P, GROUP, FEATURES], BF16, name="x_tile%d" % first)
+            nc.sync.dma_start(out=x_tile[:], in_=s_z2[:, first : first + GROUP, :])
+            x_tiles.append(x_tile)
+
+        ident = const.tile([P, P], BF16)
+        make_identity(nc, ident[:])
+        ones = const.tile([P, 1], BF16)
+        nc.vector.memset(ones[:], 1.0)
+        eps = const.tile([P, 1], F32)
+        nc.vector.memset(eps[:], EPS)
+        first_call = const.tile([P, 1], F32)
+        nc.scalar.activation(out=first_call[:], in_=eps[:], func=ACT.Sqrt)
+
+        def transpose_weight(raw, label):
+            grouped = const.tile([P, PASSES, OUT, PACK], BF16, name="%s_grouped" % label, align_bytes=64)
+            banks = []
+            for h in range(HALVES):
+                w_t = psum_x.tile([P, CHUNKS, P], BF16, tag="xt")
+                banks.append(w_t)
+            for g in range(PASSES):
+                for h in range(HALVES):
+                    for c in range(g * PACK, (g + 1) * PACK):
+                        nc.tensor.transpose(banks[h][:, c, :], raw[:, h, c * P : (c + 1) * P], ident[:])
+            for h in range(HALVES):
+                for g in range(PASSES):
+                    dst = grouped[:, g, h * P : (h + 1) * P, :]
+                    src = banks[h][:, g * PACK : (g + 1) * PACK, :].rearrange("p t n -> p n t")
+                    if h == 0:
+                        nc.vector.tensor_copy(out=dst, in_=src)
+                    else:
+                        nc.scalar.copy(out=dst, in_=src)
+            return grouped
+
+        def quantise_weight(grouped, label):
+            codes = const.tile([P, PASSES, OUT], U32, name="%s_codes" % label, align_bytes=64)
+            scales = const.tile([P, PASSES, OUT], U8, name="%s_scales" % label, align_bytes=64)
+            nc.vector.quantize_mx(
+                out=codes[:].rearrange("p g n -> p (g n)").bitcast(FP8X4),
+                scales=scales[:].rearrange("p g n -> p (g n)"),
+                in_=grouped[:].rearrange("p g n t -> p (g n t)"),
+            )
+            return codes, scales
+
+        c_w_grouped = transpose_weight(c_w_raw, "c_w")
+        s_w_grouped = transpose_weight(s_w_raw, "s_w")
+        c_w = quantise_weight(c_w_grouped, "c_w")
+        s_w = quantise_weight(s_w_grouped, "s_w")
+
+        vec_t = psum_x.tile([P, CHUNKS, P], BF16, tag="xt")
+        nc.tensor.transpose(vec_t[:, 0, :], vec_rows[:], ident[:])
+        params = const.tile([P, 4, CHUNKS], F32)
+        nc.vector.tensor_copy(
+            out=params[:].rearrange("p r c -> p (r c)"), in_=vec_t[:, 0, 0 : 4 * CHUNKS]
+        )
+
+        jobs = [{"x": [c_x[:]], "gain": params[:, 2, :], "shift": params[:, 3, :], "w": c_w}]
+        for first in range(0, SLICES, GROUP):
+            jobs.append(
+                {
+                    "x": [x_tiles[first // GROUP][:, s, :] for s in range(GROUP)],
+                    "gain": params[:, 0, :],
+                    "shift": params[:, 1, :],
+                    "w": s_w,
+                    "first": first,
+                }
+            )
+        gate = const.tile([P, OUT], F32)
+        gated_bias = const.tile([P, OUT], F32)
+        run_max = const.tile([P, GROUP, OUT], F32)
+
+        def live(j):
+            return 0 <= j < JOBS
+
+        def over_slices(vec, n):
+            return vec.unsqueeze(1).to_broadcast([P, n, CHUNKS])
+
+        def transpose_and_sum(j):
+            if not live(j):
+                return
+            job = jobs[j]
+            job["banks"] = []
+            for x in job["x"]:
+                x_t = psum_x.tile([P, CHUNKS, P], BF16, tag="xt")
+                job["banks"].append(x_t)
+            for g in range(PASSES):
+                for x, x_t in zip(job["x"], job["banks"]):
+                    for c in range(g * PACK, (g + 1) * PACK):
+                        nc.tensor.transpose(x_t[:, c, :], x[:, c * P : (c + 1) * P], ident[:])
+            sums = psum_sum.tile([P, GROUP, CHUNKS], F32)
+            for s, x in enumerate(job["x"]):
+                for c in range(CHUNKS):
+                    nc.tensor.matmul(
+                        out=sums[:, s, c : c + 1],
+                        lhsT=x[:, c * P : (c + 1) * P],
+                        rhs=ones[:],
+                        start=True,
+                        stop=True,
+                    )
+            job["sums"] = sums
+
+        def mean(j):
+            if not live(j):
+                return
+            job = jobs[j]
+            n = len(job["x"])
+            neg_mean = small.tile([P, GROUP, CHUNKS], F32)
+            nc.scalar.mul(out=neg_mean[:, :n, :], in_=job["sums"][:, :n, :], mul=-1.0 / P)
+            job["neg_mean"] = neg_mean
+
+        def deviations(j):
+            if not live(j):
+                return
+            job = jobs[j]
+            n = len(job["x"])
+            dev2 = small.tile([P, GROUP, CHUNKS], F32)
+            for s in range(n):
+                for c in range(CHUNKS):
+                    squares = work.tile([P, P], BF16)
+                    nc.scalar.activation(
+                        out=squares[:],
+                        in_=job["banks"][s][:, c, :],
+                        func=ACT.Square,
+                        bias=job["neg_mean"][:, s, c : c + 1],
+                        scale=1.0,
+                        accum_out=dev2[:, s, c : c + 1],
+                    )
+            std = small.tile([P, GROUP, CHUNKS], F32)
+            nc.scalar.activation(
+                out=std[:, :n, :], in_=dev2[:, :n, :], func=ACT.Sqrt, bias=eps[:], scale=1.0 / P
+            )
+            job["std"] = std
+
+        def inverse_std(j):
+            if not live(j):
+                return
+            job = jobs[j]
+            n = len(job["x"])
+            a = small.tile([P, GROUP, CHUNKS], F32)
+            nc.vector.reciprocal(out=a[:, :n, :], in_=job["std"][:, :n, :])
+            job["a"] = a
+
+        def scale(j):
+            if not live(j):
+                return
+            job = jobs[j]
+            n = len(job["x"])
+            a = job["a"]
+            nc.vector.tensor_tensor(out=a[:, :n, :], in0=a[:, :n, :], in1=over_slices(job["gain"], n), op=ALU.mult)
+
+        def mean_times_scale(j):
+            if not live(j):
+                return
+            job = jobs[j]
+            n = len(job["x"])
+            b = small.tile([P, GROUP, CHUNKS], F32)
+            nc.vector.tensor_tensor(out=b[:, :n, :], in0=job["neg_mean"][:, :n, :], in1=job["a"][:, :n, :], op=ALU.mult)
+            job["b"] = b
+
+        def shift(j):
+            if not live(j):
+                return
+            job = jobs[j]
+            n = len(job["x"])
+            b = job["b"]
+            nc.vector.tensor_tensor(out=b[:, :n, :], in0=b[:, :n, :], in1=over_slices(job["shift"], n), op=ALU.add)
+
+        def normalise(j):
+            if not live(j):
+                return
+            job = jobs[j]
+            planes = work.tile([P, GROUP, CHUNKS, P], BF16)
+            for s in range(len(job["x"])):
+                for c in range(CHUNKS):
+                    nc.vector.tensor_scalar(
+                        out=planes[:, s, c, :],
+                        in0=job["banks"][s][:, c, :],
+                        scalar1=job["a"][:, s, c : c + 1],
+                        scalar2=job["b"][:, s, c : c + 1],
+                        op0=ALU.mult,
+                        op1=ALU.add,
+                    )
+            job["planes"] = planes
+
+        def regroup_views(job, s, g):
+            dst = job["grouped"][:, s, g, :, :].rearrange("p (q i) t -> p q t i", i=4)
+            src = job["planes"][:, s, g * PACK : (g + 1) * PACK, :].rearrange("p t (q i) -> p q t i", i=4)
+            return dst, src
+
+        def blocks(job):
+            return [(s, g) for s in range(len(job["x"])) for g in range(PASSES)]
+
+        def regroup_on_vector(j):
+            if not live(j):
+                return
+            job = jobs[j]
+            grouped = work.tile([P, GROUP, PASSES, P, PACK], BF16, align_bytes=64)
+            job["grouped"] = grouped
+            for s, g in blocks(job)[:-1]:
+                dst, src = regroup_views(job, s, g)
+                nc.vector.tensor_scalar_max(out=dst, in0=src, scalar1=0.0)
+
+        def regroup_on_scalar(j):
+            if not live(j):
+                return
+            job = jobs[j]
+            s, g = blocks(job)[-1]
+            dst, src = regroup_views(job, s, g)
+            nc.scalar.activation(out=dst, in_=src, func=ACT.Relu)
+
+        def quantise(j):
+            if not live(j):
+                return
+            job = jobs[j]
+            n = len(job["x"])
+            codes = work.tile([P, GROUP, PASSES, P], U32, align_bytes=64)
+            scales = work.tile([P, GROUP, PASSES, P], U8, align_bytes=64)
+            nc.vector.quantize_mx(
+                out=codes[:, :n, :, :].rearrange("p s g m -> p (s g m)").bitcast(FP8X4),
+                scales=scales[:, :n, :, :].rearrange("p s g m -> p (s g m)"),
+                in_=job["grouped"][:, :n, :, :, :].rearrange("p s g m t -> p (s g m t)"),
+            )
+            job["codes"] = codes
+            job["scales"] = scales
+
+        def project(j):
+            if not live(j):
+                return
+            job = jobs[j]
+            w_codes, w_scales = job["w"]
+            acc = psum_acc.tile([P, GROUP, OUT], F32)
+            for s in range(len(job["x"])):
+                for g in range(PASSES):
+                    nc.tensor.matmul_mx(
+                        out=acc[:, s, :],
+                        lhsT=job["codes"][:, s, g, :].bitcast(FP8X4),
+                        lhsT_scale=job["scales"][:, s, g, :],
+                        rhs=w_codes[:, g, :].bitcast(FP8X4),
+                        rhs_scale=w_scales[:, g, :],
+                        start=(g == 0),
+                        stop=(g == PASSES - 1),
+                    )
+            job["acc"] = acc
+
+        def apply_gate(j, s):
+            if not live(j):
+                return
+            job = jobs[j]
+            if j == 0:
+                if s == 0:
+                    nc.vector.tensor_tensor(out=gate[:], in0=job["acc"][:, 0, :], in1=c_bias[:], op=ALU.add)
+                else:
+                    nc.vector.tensor_tensor(out=gated_bias[:], in0=gate[:], in1=s_bias[:], op=ALU.mult)
+                return
+            if s == 0:
+                gated = work.tile([P, GROUP, OUT], F32)
+                job["gated"] = gated
+            nc.vector.tensor_tensor(out=job["gated"][:, s, :], in0=job["acc"][:, s, :], in1=gate[:], op=ALU.mult)
+
+        def add_bias_and_store(j):
+            if not 1 <= j < JOBS:
+                return
+            job = jobs[j]
+            result = results.tile([P, GROUP, OUT], F32)
+            for s in range(GROUP):
+                nc.gpsimd.tensor_tensor(out=result[:, s, :], in0=job["gated"][:, s, :], in1=gated_bias[:], op=ALU.add)
+            nc.sync.dma_start(out=out_0[:, job["first"] : job["first"] + GROUP, :], in_=result[:])
+
+        def pool(j):
+            if not 1 <= j < JOBS:
+                return
+            if j == 1:
+                nc.vector.tensor_copy(out=run_max[:], in_=jobs[j]["gated"][:])
+            else:
+                nc.vector.tensor_tensor(out=run_max[:], in0=run_max[:], in1=jobs[j]["gated"][:], op=ALU.max)
+
+        for k in range(-2, JOBS + 3):
+            project(k - 2)
+            inverse_std(k)
+            pool(k - 3)
+            scale(k)
+            quantise(k - 1)
+            mean_times_scale(k)
+            apply_gate(k - 2, 0)
+            shift(k)
+            apply_gate(k - 2, 1)
+            add_bias_and_store(k - 2)
+            deviations(k + 1)
+            normalise(k)
+            regroup_on_vector(k)
+            transpose_and_sum(k + 2)
+            mean(k + 2)
+            regroup_on_scalar(k)
+
+        pooled = const.tile([P, OUT], F32)
+        nc.vector.tensor_tensor(out=pooled[:], in0=run_max[:, 0, :], in1=run_max[:, 1, :], op=ALU.max)
+        nc.vector.tensor_tensor(out=pooled[:], in0=pooled[:], in1=gated_bias[:], op=ALU.add)
+        nc.sync.dma_start(out=out_1, in_=pooled[:])

@@ -22,6 +22,7 @@ PASSES = FEATURES // (P * PACK)
 GROUP = 2
 JOBS = 1 + SLICES // GROUP
 HALVES = OUT // P
+RUN = 8
 
 FLOPS = 2 * (SLICES + 1) * P * FEATURES * OUT
 
@@ -243,8 +244,8 @@ def tile_cgblock_pb_t_kernel(
             job["planes"] = planes
 
         def regroup_views(job, s, g):
-            dst = job["grouped"][:, s, g, :, :].rearrange("p (q i) t -> p q t i", i=4)
-            src = job["planes"][:, s, g * PACK : (g + 1) * PACK, :].rearrange("p t (q i) -> p q t i", i=4)
+            dst = job["grouped"][:, s, g, :, :].rearrange("p (q i) t -> p q t i", i=RUN)
+            src = job["planes"][:, s, g * PACK : (g + 1) * PACK, :].rearrange("p t (q i) -> p q t i", i=RUN)
             return dst, src
 
         def blocks(job):

@@ -22,6 +22,7 @@ PASSES = FEATURES // (P * PACK)
 GROUP = 2
 JOBS = 1 + SLICES // GROUP
 HALVES = OUT // P
+SCALAR_ROWS = 32
 RUN = 8
 
 FLOPS = 2 * (SLICES + 1) * P * FEATURES * OUT
@@ -243,13 +244,21 @@ def tile_cgblock_pb_t_kernel(
                     )
             job["planes"] = planes
 
-        def regroup_views(job, s, g):
-            dst = job["grouped"][:, s, g, :, :].rearrange("p (q i) t -> p q t i", i=RUN)
-            src = job["planes"][:, s, g * PACK : (g + 1) * PACK, :].rearrange("p t (q i) -> p q t i", i=RUN)
+        def regroup_views(job, s, g, rows):
+            dst = job["grouped"][:, s, g, rows, :].rearrange("p (q i) t -> p q t i", i=RUN)
+            src = job["planes"][:, s, g * PACK : (g + 1) * PACK, rows].rearrange("p t (q i) -> p q t i", i=RUN)
             return dst, src
 
         def blocks(job):
             return [(s, g) for s in range(len(job["x"])) for g in range(PASSES)]
+
+        def vector_share(job):
+            *whole, (s, g), _ = blocks(job)
+            return [(b[0], b[1], slice(0, P)) for b in whole] + [(s, g, slice(0, P - SCALAR_ROWS))]
+
+        def scalar_share(job):
+            *_, (s, g), (s_last, g_last) = blocks(job)
+            return [(s, g, slice(P - SCALAR_ROWS, P)), (s_last, g_last, slice(0, P))]
 
         def regroup_on_vector(j):
             if not live(j):
@@ -257,17 +266,17 @@ def tile_cgblock_pb_t_kernel(
             job = jobs[j]
             grouped = work.tile([P, GROUP, PASSES, P, PACK], BF16, align_bytes=64)
             job["grouped"] = grouped
-            for s, g in blocks(job)[:-1]:
-                dst, src = regroup_views(job, s, g)
+            for s, g, rows in vector_share(job):
+                dst, src = regroup_views(job, s, g, rows)
                 nc.vector.tensor_scalar_max(out=dst, in0=src, scalar1=0.0)
 
         def regroup_on_scalar(j):
             if not live(j):
                 return
             job = jobs[j]
-            s, g = blocks(job)[-1]
-            dst, src = regroup_views(job, s, g)
-            nc.scalar.activation(out=dst, in_=src, func=ACT.Relu)
+            for s, g, rows in scalar_share(job):
+                dst, src = regroup_views(job, s, g, rows)
+                nc.scalar.activation(out=dst, in_=src, func=ACT.Relu)
 
         def quantise(j):
             if not live(j):

@@ -42,23 +42,25 @@ def tile_cgblock_pb_t_kernel(
         psum_sum = stack.enter_context(tc.psum_pool(name="psum_sum", bufs=1))
         psum_acc = stack.enter_context(tc.psum_pool(name="psum_acc", bufs=1))
 
+        blank = const.tile([P, OUT], BF16)
+        nc.vector.memset(blank[:], 0.0)
         vec_rows = const.tile([P, P], BF16)
         nc.vector.memset(vec_rows[:], 0.0)
+        bias_rows = const.tile([P, 2, OUT], BF16)
+        nc.vector.memset(bias_rows[:], 0.0)
         for r, vec in enumerate((s_g2, s_be2, c_g2, c_be2)):
             nc.scalar.dma_start(
                 out=vec_rows[r * CHUNKS : (r + 1) * CHUNKS, :],
                 in_=vec.rearrange("(c p) -> c p", p=P),
             )
+        for r, vec in enumerate((c_b3, s_b3)):
+            nc.scalar.dma_start(out=bias_rows[0:1, r, :], in_=vec.unsqueeze(0))
         c_w_raw = const.tile([P, HALVES, FEATURES], BF16)
         nc.sync.dma_start(out=c_w_raw[:], in_=c_w3.rearrange("(h n) k -> n h k", n=P))
-        s_w_raw = const.tile([P, HALVES, FEATURES], BF16)
-        nc.sync.dma_start(out=s_w_raw[:], in_=s_w3.rearrange("(h n) k -> n h k", n=P))
         c_x = const.tile([P, FEATURES], BF16)
         nc.sync.dma_start(out=c_x[:], in_=c_z2)
-        c_bias = const.tile([P, OUT], BF16)
-        nc.scalar.dma_start(out=c_bias[:], in_=c_b3.partition_broadcast(P))
-        s_bias = const.tile([P, OUT], BF16)
-        nc.scalar.dma_start(out=s_bias[:], in_=s_b3.partition_broadcast(P))
+        s_w_raw = const.tile([P, HALVES, FEATURES], BF16)
+        nc.sync.dma_start(out=s_w_raw[:], in_=s_w3.rearrange("(h n) k -> n h k", n=P))
         x_tiles = []
         for first in range(0, SLICES, GROUP):
             x_tile = const.tile([P, GROUP, FEATURES], BF16, name="x_tile%d" % first)
@@ -67,12 +69,16 @@ def tile_cgblock_pb_t_kernel(
 
         ident = const.tile([P, P], BF16)
         make_identity(nc, ident[:])
-        ones = const.tile([P, 1], BF16)
+        ones = const.tile([P, P], BF16)
         nc.vector.memset(ones[:], 1.0)
         eps = const.tile([P, 1], F32)
         nc.vector.memset(eps[:], EPS)
         first_call = const.tile([P, 1], F32)
         nc.scalar.activation(out=first_call[:], in_=eps[:], func=ACT.Sqrt)
+
+        def raise_clock(passes, bank):
+            for r in range(passes):
+                nc.tensor.matmul(out=bank[:, OUT : 2 * OUT], lhsT=blank[:, 0:P], rhs=blank[:], start=True, stop=True)
 
         def transpose_weight(raw, label):
             grouped = const.tile([P, PASSES, OUT, PACK], BF16, name="%s_grouped" % label, align_bytes=64)
@@ -104,26 +110,16 @@ def tile_cgblock_pb_t_kernel(
             )
             return codes, scales
 
-        c_w_grouped = transpose_weight(c_w_raw, "c_w")
-        s_w_grouped = transpose_weight(s_w_raw, "s_w")
-        c_w = quantise_weight(c_w_grouped, "c_w")
-        s_w = quantise_weight(s_w_grouped, "s_w")
-
-        vec_t = psum_x.tile([P, CHUNKS, P], BF16, tag="xt")
-        nc.tensor.transpose(vec_t[:, 0, :], vec_rows[:], ident[:])
         params = const.tile([P, 4, CHUNKS], F32)
-        nc.vector.tensor_copy(
-            out=params[:].rearrange("p r c -> p (r c)"), in_=vec_t[:, 0, 0 : 4 * CHUNKS]
-        )
-
-        jobs = [{"x": [c_x[:]], "gain": params[:, 2, :], "shift": params[:, 3, :], "w": c_w}]
+        biases = const.tile([P, 2, OUT], F32)
+        c_bias, s_bias = biases[:, 0, :], biases[:, 1, :]
+        jobs = [{"x": [c_x[:]], "gain": params[:, 2, :], "shift": params[:, 3, :]}]
         for first in range(0, SLICES, GROUP):
             jobs.append(
                 {
                     "x": [x_tiles[first // GROUP][:, s, :] for s in range(GROUP)],
                     "gain": params[:, 0, :],
                     "shift": params[:, 1, :],
-                    "w": s_w,
                     "first": first,
                 }
             )
@@ -149,13 +145,15 @@ def tile_cgblock_pb_t_kernel(
                 for x, x_t in zip(job["x"], job["banks"]):
                     for c in range(g * PACK, (g + 1) * PACK):
                         nc.tensor.transpose(x_t[:, c, :], x[:, c * P : (c + 1) * P], ident[:])
-            sums = psum_sum.tile([P, GROUP, CHUNKS], F32)
+            sums_bank = psum_sum.tile([P, 2 * OUT], F32, tag="sums")
+            sums = sums_bank[:, 0 : GROUP * CHUNKS].rearrange("p (s c) -> p s c", c=CHUNKS)
+            job["sums_bank"] = sums_bank
             for s, x in enumerate(job["x"]):
                 for c in range(CHUNKS):
                     nc.tensor.matmul(
                         out=sums[:, s, c : c + 1],
                         lhsT=x[:, c * P : (c + 1) * P],
-                        rhs=ones[:],
+                        rhs=ones[:, 0:1],
                         start=True,
                         stop=True,
                     )
@@ -297,8 +295,8 @@ def tile_cgblock_pb_t_kernel(
             if not live(j):
                 return
             job = jobs[j]
-            w_codes, w_scales = job["w"]
-            acc = psum_acc.tile([P, GROUP, OUT], F32)
+            w_codes, w_scales = c_w if j == 0 else s_w
+            acc = psum_acc.tile([P, GROUP, OUT], F32, tag="acc")
             for s in range(len(job["x"])):
                 for g in range(PASSES):
                     nc.tensor.matmul_mx(
@@ -318,9 +316,9 @@ def tile_cgblock_pb_t_kernel(
             job = jobs[j]
             if j == 0:
                 if s == 0:
-                    nc.vector.tensor_tensor(out=gate[:], in0=job["acc"][:, 0, :], in1=c_bias[:], op=ALU.add)
+                    nc.vector.tensor_tensor(out=gate[:], in0=job["acc"][:, 0, :], in1=c_bias, op=ALU.add)
                 else:
-                    nc.vector.tensor_tensor(out=gated_bias[:], in0=gate[:], in1=s_bias[:], op=ALU.mult)
+                    nc.vector.tensor_tensor(out=gated_bias[:], in0=gate[:], in1=s_bias, op=ALU.mult)
                 return
             if s == 0:
                 gated = work.tile([P, GROUP, OUT], F32)
@@ -344,7 +342,35 @@ def tile_cgblock_pb_t_kernel(
             else:
                 nc.vector.tensor_tensor(out=run_max[:], in0=run_max[:], in1=jobs[j]["gated"][:], op=ALU.max)
 
-        for k in range(-2, JOBS + 3):
+        head_bank = psum_sum.tile([P, 2 * OUT], F32, tag="sums")
+        raise_clock(10, head_bank)
+        c_w_grouped = transpose_weight(c_w_raw, "c_w")
+        raise_clock(4, head_bank)
+        transpose_and_sum(0)
+        mean(0)
+        deviations(0)
+
+        bias_bank = psum_acc.tile([P, 2 * OUT], F32, tag="acc")
+        nc.tensor.matmul(
+            out=bias_bank[:], lhsT=ones[:], rhs=bias_rows[:].rearrange("p r n -> p (r n)"), start=True, stop=True
+        )
+        nc.scalar.copy(out=biases[:].rearrange("p r n -> p (r n)"), in_=bias_bank[:])
+
+        vec_t = psum_x.tile([P, CHUNKS, P], BF16, tag="xt")
+        nc.tensor.transpose(vec_t[:, 0, :], vec_rows[:], ident[:])
+        nc.vector.tensor_copy(
+            out=params[:].rearrange("p r c -> p (r c)"), in_=vec_t[:, 0, 0 : 4 * CHUNKS]
+        )
+
+        s_w_grouped = transpose_weight(s_w_raw, "s_w")
+        raise_clock(4, jobs[0]["sums_bank"])
+        c_w = quantise_weight(c_w_grouped, "c_w")
+        s_w = quantise_weight(s_w_grouped, "s_w")
+        transpose_and_sum(1)
+        mean(1)
+        raise_clock(4, jobs[1]["sums_bank"])
+
+        for k in range(JOBS + 3):
             project(k - 2)
             inverse_std(k)
             pool(k - 3)

@@ -56,16 +56,24 @@ def tile_cgblock_pb_t_kernel(
         for r, vec in enumerate((c_b3, s_b3)):
             nc.scalar.dma_start(out=bias_rows[0:1, r, :], in_=vec.unsqueeze(0))
         c_w_raw = const.tile([P, HALVES, FEATURES], BF16)
-        nc.sync.dma_start(out=c_w_raw[:], in_=c_w3.rearrange("(h n) k -> n h k", n=P))
         c_x = const.tile([P, FEATURES], BF16)
-        nc.sync.dma_start(out=c_x[:], in_=c_z2)
         s_w_raw = const.tile([P, HALVES, FEATURES], BF16)
-        nc.sync.dma_start(out=s_w_raw[:], in_=s_w3.rearrange("(h n) k -> n h k", n=P))
-        x_tiles = []
-        for first in range(0, SLICES, GROUP):
-            x_tile = const.tile([P, GROUP, FEATURES], BF16, name="x_tile%d" % first)
-            nc.sync.dma_start(out=x_tile[:], in_=s_z2[:, first : first + GROUP, :])
-            x_tiles.append(x_tile)
+        x_tiles = [const.tile([P, GROUP, FEATURES], BF16, name="x_tile%d" % r) for r in range(SLICES // GROUP)]
+
+        def load_weight(raw, w, h):
+            nc.sync.dma_start(out=raw[:, h, :], in_=w[h * P : (h + 1) * P, :])
+
+        def load_slices(r):
+            nc.sync.dma_start(out=x_tiles[r][:], in_=s_z2[:, r * GROUP : (r + 1) * GROUP, :])
+
+        load_weight(c_w_raw, c_w3, 0)
+        nc.sync.dma_start(out=c_x[:], in_=c_z2)
+        load_weight(c_w_raw, c_w3, 1)
+        load_slices(0)
+        for h in range(HALVES):
+            load_weight(s_w_raw, s_w3, h)
+        for r in range(1, SLICES // GROUP):
+            load_slices(r)
 
         ident = const.tile([P, P], BF16)
         make_identity(nc, ident[:])
@@ -80,35 +88,34 @@ def tile_cgblock_pb_t_kernel(
             for r in range(passes):
                 nc.tensor.matmul(out=bank[:, OUT : 2 * OUT], lhsT=blank[:, 0:P], rhs=blank[:], start=True, stop=True)
 
-        def transpose_weight(raw, label):
+        def new_weight(raw, label):
             grouped = const.tile([P, PASSES, OUT, PACK], BF16, name="%s_grouped" % label, align_bytes=64)
-            banks = []
-            for h in range(HALVES):
-                w_t = psum_x.tile([P, CHUNKS, P], BF16, tag="xt")
-                banks.append(w_t)
-            for g in range(PASSES):
-                for h in range(HALVES):
-                    for c in range(g * PACK, (g + 1) * PACK):
-                        nc.tensor.transpose(banks[h][:, c, :], raw[:, h, c * P : (c + 1) * P], ident[:])
-            for h in range(HALVES):
-                for g in range(PASSES):
-                    dst = grouped[:, g, h * P : (h + 1) * P, :]
-                    src = banks[h][:, g * PACK : (g + 1) * PACK, :].rearrange("p t n -> p n t")
-                    if h == 0:
-                        nc.vector.tensor_copy(out=dst, in_=src)
-                    else:
-                        nc.scalar.copy(out=dst, in_=src)
-            return grouped
-
-        def quantise_weight(grouped, label):
             codes = const.tile([P, PASSES, OUT], U32, name="%s_codes" % label, align_bytes=64)
             scales = const.tile([P, PASSES, OUT], U8, name="%s_scales" % label, align_bytes=64)
+            return {"raw": raw, "grouped": grouped, "codes": codes, "scales": scales, "banks": {}}
+
+        def transpose_weight(weight, h):
+            w_t = psum_x.tile([P, CHUNKS, P], BF16, tag="xt")
+            for c in range(CHUNKS):
+                nc.tensor.transpose(w_t[:, c, :], weight["raw"][:, h, c * P : (c + 1) * P], ident[:])
+            weight["banks"][h] = w_t
+
+        def regroup_weight(weight, h):
+            for g in range(PASSES):
+                nc.vector.tensor_copy(
+                    out=weight["grouped"][:, g, h * P : (h + 1) * P, :],
+                    in_=weight["banks"][h][:, g * PACK : (g + 1) * PACK, :].rearrange("p t n -> p n t"),
+                )
+
+        def quantise_weight(weight):
             nc.vector.quantize_mx(
-                out=codes[:].rearrange("p g n -> p (g n)").bitcast(FP8X4),
-                scales=scales[:].rearrange("p g n -> p (g n)"),
-                in_=grouped[:].rearrange("p g n t -> p (g n t)"),
+                out=weight["codes"][:].rearrange("p g n -> p (g n)").bitcast(FP8X4),
+                scales=weight["scales"][:].rearrange("p g n -> p (g n)"),
+                in_=weight["grouped"][:].rearrange("p g n t -> p (g n t)"),
             )
-            return codes, scales
+
+        c_w = new_weight(c_w_raw, "c_w")
+        s_w = new_weight(s_w_raw, "s_w")
 
         params = const.tile([P, 4, CHUNKS], F32)
         biases = const.tile([P, 2, OUT], F32)
@@ -295,8 +302,12 @@ def tile_cgblock_pb_t_kernel(
             if not live(j):
                 return
             job = jobs[j]
-            w_codes, w_scales = c_w if j == 0 else s_w
-            acc = psum_acc.tile([P, GROUP, OUT], F32, tag="acc")
+            weight = c_w if j == 0 else s_w
+            w_codes, w_scales = weight["codes"], weight["scales"]
+            if j == JOBS - 1:
+                acc = psum_x.tile([P, GROUP, OUT], F32, tag="xt")
+            else:
+                acc = psum_acc.tile([P, GROUP, OUT], F32, tag="acc")
             for s in range(len(job["x"])):
                 for g in range(PASSES):
                     nc.tensor.matmul_mx(
@@ -330,8 +341,9 @@ def tile_cgblock_pb_t_kernel(
                 return
             job = jobs[j]
             result = results.tile([P, GROUP, OUT], F32)
+            engine = nc.vector if j == JOBS - 1 else nc.gpsimd
             for s in range(GROUP):
-                nc.gpsimd.tensor_tensor(out=result[:, s, :], in0=job["gated"][:, s, :], in1=gated_bias[:], op=ALU.add)
+                engine.tensor_tensor(out=result[:, s, :], in0=job["gated"][:, s, :], in1=gated_bias[:], op=ALU.add)
             nc.sync.dma_start(out=out_0[:, job["first"] : job["first"] + GROUP, :], in_=result[:])
 
         def pool(j):
@@ -342,35 +354,59 @@ def tile_cgblock_pb_t_kernel(
             else:
                 nc.vector.tensor_tensor(out=run_max[:], in0=run_max[:], in1=jobs[j]["gated"][:], op=ALU.max)
 
+        def short_steps(j):
+            inverse_std(j)
+            scale(j)
+            mean_times_scale(j)
+            shift(j)
+
         head_bank = psum_sum.tile([P, 2 * OUT], F32, tag="sums")
-        raise_clock(10, head_bank)
-        c_w_grouped = transpose_weight(c_w_raw, "c_w")
-        raise_clock(4, head_bank)
+        raise_clock(12, head_bank)
+        transpose_weight(c_w, 0)
+        regroup_weight(c_w, 0)
         transpose_and_sum(0)
         mean(0)
         deviations(0)
+        transpose_weight(c_w, 1)
+        regroup_weight(c_w, 1)
+        raise_clock(4, jobs[0]["sums_bank"])
 
         bias_bank = psum_acc.tile([P, 2 * OUT], F32, tag="acc")
         nc.tensor.matmul(
             out=bias_bank[:], lhsT=ones[:], rhs=bias_rows[:].rearrange("p r n -> p (r n)"), start=True, stop=True
         )
-        nc.scalar.copy(out=biases[:].rearrange("p r n -> p (r n)"), in_=bias_bank[:])
-
         vec_t = psum_x.tile([P, CHUNKS, P], BF16, tag="xt")
         nc.tensor.transpose(vec_t[:, 0, :], vec_rows[:], ident[:])
         nc.vector.tensor_copy(
             out=params[:].rearrange("p r c -> p (r c)"), in_=vec_t[:, 0, 0 : 4 * CHUNKS]
         )
 
-        s_w_grouped = transpose_weight(s_w_raw, "s_w")
-        raise_clock(4, jobs[0]["sums_bank"])
-        c_w = quantise_weight(c_w_grouped, "c_w")
-        s_w = quantise_weight(s_w_grouped, "s_w")
         transpose_and_sum(1)
         mean(1)
-        raise_clock(4, jobs[1]["sums_bank"])
+        quantise_weight(c_w)
+        short_steps(0)
+        normalise(0)
+        regroup_on_vector(0)
+        for h in range(HALVES):
+            transpose_weight(s_w, h)
+        regroup_weight(s_w, 0)
+        deviations(1)
+        nc.scalar.copy(out=biases[:].rearrange("p r n -> p (r n)"), in_=bias_bank[:])
+        regroup_weight(s_w, 1)
+        quantise_weight(s_w)
+        transpose_and_sum(2)
+        mean(2)
+        regroup_on_scalar(0)
+        short_steps(1)
+        deviations(2)
+        normalise(1)
+        regroup_on_vector(1)
+        quantise(0)
+        transpose_and_sum(3)
+        mean(3)
+        regroup_on_scalar(1)
 
-        for k in range(JOBS + 3):
+        for k in range(2, JOBS):
             project(k - 2)
             inverse_std(k)
             pool(k - 3)
@@ -387,6 +423,19 @@ def tile_cgblock_pb_t_kernel(
             transpose_and_sum(k + 2)
             mean(k + 2)
             regroup_on_scalar(k)
+
+        project(JOBS - 2)
+        pool(JOBS - 3)
+        quantise(JOBS - 1)
+        project(JOBS - 1)
+        apply_gate(JOBS - 2, 0)
+        apply_gate(JOBS - 2, 1)
+        add_bias_and_store(JOBS - 2)
+        apply_gate(JOBS - 1, 0)
+        apply_gate(JOBS - 1, 1)
+        pool(JOBS - 2)
+        add_bias_and_store(JOBS - 1)
+        pool(JOBS - 1)
 
         pooled = const.tile([P, OUT], F32)
         nc.vector.tensor_tensor(out=pooled[:], in0=run_max[:, 0, :], in1=run_max[:, 1, :], op=ALU.max)

@@ -22,6 +22,7 @@ PASSES = FEATURES // (P * PACK)
 GROUP = 2
 JOBS = 1 + SLICES // GROUP
 HALVES = OUT // P
+PAIR = 2
 SCALAR_ROWS = 32
 RUN = 8
 
@@ -132,7 +133,8 @@ def tile_cgblock_pb_t_kernel(
             )
         gate = const.tile([P, OUT], F32)
         gated_bias = const.tile([P, OUT], F32)
-        run_max = const.tile([P, GROUP, OUT], F32)
+        run_max = const.tile([P, PAIR, OUT], F32)
+        pairs = [{} for m in range(JOBS)]
 
         def live(j):
             return 0 <= j < JOBS
@@ -331,28 +333,36 @@ def tile_cgblock_pb_t_kernel(
                 else:
                     nc.vector.tensor_tensor(out=gated_bias[:], in0=gate[:], in1=s_bias, op=ALU.mult)
                 return
-            if s == 0:
-                gated = work.tile([P, GROUP, OUT], F32)
-                job["gated"] = gated
-            nc.vector.tensor_tensor(out=job["gated"][:, s, :], in0=job["acc"][:, s, :], in1=gate[:], op=ALU.mult)
+            m, place = (j - 1, 1) if s == 0 else (j, 0)
+            if s == 1 or j == 1:
+                gated = work.tile([P, PAIR, OUT], F32)
+                pairs[m]["gated"] = gated
+            nc.vector.tensor_tensor(
+                out=pairs[m]["gated"][:, place, :], in0=job["acc"][:, s, :], in1=gate[:], op=ALU.mult
+            )
 
-        def add_bias_and_store(j):
-            if not 1 <= j < JOBS:
-                return
-            job = jobs[j]
-            result = results.tile([P, GROUP, OUT], F32)
-            engine = nc.vector if j == JOBS - 1 else nc.gpsimd
-            for s in range(GROUP):
-                engine.tensor_tensor(out=result[:, s, :], in0=job["gated"][:, s, :], in1=gated_bias[:], op=ALU.add)
-            nc.sync.dma_start(out=out_0[:, job["first"] : job["first"] + GROUP, :], in_=result[:])
+        def places(m):
+            return slice(1 if m == 0 else 0, 1 if m == JOBS - 1 else PAIR)
 
-        def pool(j):
-            if not 1 <= j < JOBS:
+        def add_bias_and_store(m, engine):
+            if not 0 <= m < JOBS:
                 return
-            if j == 1:
-                nc.vector.tensor_copy(out=run_max[:], in_=jobs[j]["gated"][:])
+            held = places(m)
+            result = results.tile([P, PAIR, OUT], F32)
+            bias = gated_bias[:].unsqueeze(1).to_broadcast([P, held.stop - held.start, OUT])
+            engine.tensor_tensor(out=result[:, held, :], in0=pairs[m]["gated"][:, held, :], in1=bias, op=ALU.add)
+            first = PAIR * m - 1
+            nc.sync.dma_start(out=out_0[:, first + held.start : first + held.stop, :], in_=result[:, held, :])
+
+        def pool(m):
+            if not 0 <= m < JOBS:
+                return
+            gated = pairs[m]["gated"]
+            if m == 0:
+                nc.vector.tensor_copy(out=run_max[:], in_=gated[:, 1, :].unsqueeze(1).to_broadcast([P, PAIR, OUT]))
             else:
-                nc.vector.tensor_tensor(out=run_max[:], in0=run_max[:], in1=jobs[j]["gated"][:], op=ALU.max)
+                held = places(m)
+                nc.vector.tensor_tensor(out=run_max[:, held, :], in0=run_max[:, held, :], in1=gated[:, held, :], op=ALU.max)
 
         def short_steps(j):
             inverse_std(j)
@@ -409,14 +419,14 @@ def tile_cgblock_pb_t_kernel(
         for k in range(2, JOBS):
             project(k - 2)
             inverse_std(k)
-            pool(k - 3)
+            pool(k - 4)
             scale(k)
             quantise(k - 1)
             mean_times_scale(k)
             apply_gate(k - 2, 0)
             shift(k)
             apply_gate(k - 2, 1)
-            add_bias_and_store(k - 2)
+            add_bias_and_store(k - 3, nc.gpsimd)
             deviations(k + 1)
             normalise(k)
             regroup_on_vector(k)
@@ -424,18 +434,21 @@ def tile_cgblock_pb_t_kernel(
             mean(k + 2)
             regroup_on_scalar(k)
 
-        project(JOBS - 2)
-        pool(JOBS - 3)
-        quantise(JOBS - 1)
-        project(JOBS - 1)
-        apply_gate(JOBS - 2, 0)
-        apply_gate(JOBS - 2, 1)
-        add_bias_and_store(JOBS - 2)
-        apply_gate(JOBS - 1, 0)
-        apply_gate(JOBS - 1, 1)
-        pool(JOBS - 2)
-        add_bias_and_store(JOBS - 1)
-        pool(JOBS - 1)
+        last = JOBS - 1
+        project(last - 1)
+        pool(last - 3)
+        quantise(last)
+        project(last)
+        apply_gate(last - 1, 0)
+        apply_gate(last - 1, 1)
+        add_bias_and_store(last - 2, nc.gpsimd)
+        apply_gate(last, 0)
+        apply_gate(last, 1)
+        add_bias_and_store(last - 1, nc.vector)
+        pool(last - 2)
+        add_bias_and_store(last, nc.vector)
+        pool(last - 1)
+        pool(last)
 
         pooled = const.tile([P, OUT], F32)
         nc.vector.tensor_tensor(out=pooled[:], in0=run_max[:, 0, :], in1=run_max[:, 1, :], op=ALU.max)

@@ -241,14 +241,12 @@ def tile_cgblock_pb_t_kernel(
             planes = work.tile([P, GROUP, CHUNKS, P], BF16)
             for s in range(len(job["x"])):
                 for c in range(CHUNKS):
-                    nc.vector.tensor_scalar(
-                        out=planes[:, s, c, :],
-                        in0=job["banks"][s][:, c, :],
-                        scalar1=job["a"][:, s, c : c + 1],
-                        scalar2=job["b"][:, s, c : c + 1],
-                        op0=ALU.mult,
-                        op1=ALU.add,
-                    )
+                    out, x = planes[:, s, c, :], job["banks"][s][:, c, :]
+                    a, b = job["a"][:, s, c : c + 1], job["b"][:, s, c : c + 1]
+                    if j == JOBS - 1 and s == 1:
+                        nc.scalar.activation(out=out, in_=x, func=ACT.Identity, bias=b, scale=a)
+                    else:
+                        nc.vector.tensor_scalar(out=out, in0=x, scalar1=a, scalar2=b, op0=ALU.mult, op1=ALU.add)
             job["planes"] = planes
 
         def regroup_views(job, s, g, rows):
@@ -259,31 +257,29 @@ def tile_cgblock_pb_t_kernel(
         def blocks(job):
             return [(s, g) for s in range(len(job["x"])) for g in range(PASSES)]
 
-        def vector_share(job):
-            *whole, (s, g), _ = blocks(job)
-            return [(b[0], b[1], slice(0, P)) for b in whole] + [(s, g, slice(0, P - SCALAR_ROWS))]
+        def scalar_rows(j):
+            return 0 if j == JOBS - 1 else SCALAR_ROWS
 
-        def scalar_share(job):
-            *_, (s, g), (s_last, g_last) = blocks(job)
-            return [(s, g, slice(P - SCALAR_ROWS, P)), (s_last, g_last, slice(0, P))]
-
-        def regroup_on_vector(j):
+        def regroup_on_vector(j, which):
             if not live(j):
                 return
             job = jobs[j]
-            grouped = work.tile([P, GROUP, PASSES, P, PACK], BF16, align_bytes=64)
-            job["grouped"] = grouped
-            for s, g, rows in vector_share(job):
-                dst, src = regroup_views(job, s, g, rows)
+            if "grouped" not in job:
+                job["grouped"] = work.tile([P, GROUP, PASSES, P, PACK], BF16, align_bytes=64, name="grouped")
+            shared = blocks(job)[-2]
+            for s, g in blocks(job)[:-1][which]:
+                dst, src = regroup_views(job, s, g, slice(0, P - scalar_rows(j) if (s, g) == shared else P))
                 nc.vector.tensor_scalar_max(out=dst, in0=src, scalar1=0.0)
 
         def regroup_on_scalar(j):
             if not live(j):
                 return
             job = jobs[j]
-            for s, g, rows in scalar_share(job):
-                dst, src = regroup_views(job, s, g, rows)
-                nc.scalar.activation(out=dst, in_=src, func=ACT.Relu)
+            shared, own = blocks(job)[-2:]
+            for (s, g), rows in ((shared, slice(P - scalar_rows(j), P)), (own, slice(0, P))):
+                if rows.start < rows.stop:
+                    dst, src = regroup_views(job, s, g, rows)
+                    nc.scalar.activation(out=dst, in_=src, func=ACT.Relu)
 
         def quantise(j):
             if not live(j):
@@ -364,6 +360,8 @@ def tile_cgblock_pb_t_kernel(
                 held = places(m)
                 nc.vector.tensor_tensor(out=run_max[:, held, :], in0=run_max[:, held, :], in1=gated[:, held, :], op=ALU.max)
 
+        every, early, late = slice(None), slice(0, -1), slice(-1, None)
+
         def short_steps(j):
             inverse_std(j)
             scale(j)
@@ -396,7 +394,7 @@ def tile_cgblock_pb_t_kernel(
         quantise_weight(c_w)
         short_steps(0)
         normalise(0)
-        regroup_on_vector(0)
+        regroup_on_vector(0, every)
         for h in range(HALVES):
             transpose_weight(s_w, h)
         regroup_weight(s_w, 0)
@@ -410,7 +408,7 @@ def tile_cgblock_pb_t_kernel(
         short_steps(1)
         deviations(2)
         normalise(1)
-        regroup_on_vector(1)
+        regroup_on_vector(1, every)
         quantise(0)
         transpose_and_sum(3)
         mean(3)
@@ -429,7 +427,7 @@ def tile_cgblock_pb_t_kernel(
             add_bias_and_store(k - 3, nc.gpsimd)
             deviations(k + 1)
             normalise(k)
-            regroup_on_vector(k)
+            regroup_on_vector(k, early if k == JOBS - 1 else every)
             transpose_and_sum(k + 2)
             mean(k + 2)
             regroup_on_scalar(k)
@@ -437,6 +435,7 @@ def tile_cgblock_pb_t_kernel(
         last = JOBS - 1
         project(last - 1)
         pool(last - 3)
+        regroup_on_vector(last, late)
         quantise(last)
         project(last)
         apply_gate(last - 1, 0)
@@ -444,13 +443,15 @@ def tile_cgblock_pb_t_kernel(
         add_bias_and_store(last - 2, nc.gpsimd)
         apply_gate(last, 0)
         apply_gate(last, 1)
-        add_bias_and_store(last - 1, nc.vector)
         pool(last - 2)
-        add_bias_and_store(last, nc.vector)
+        add_bias_and_store(last - 1, nc.vector)
         pool(last - 1)
+        add_bias_and_store(last, nc.vector)
         pool(last)
-
         pooled = const.tile([P, OUT], F32)
-        nc.vector.tensor_tensor(out=pooled[:], in0=run_max[:, 0, :], in1=run_max[:, 1, :], op=ALU.max)
-        nc.vector.tensor_tensor(out=pooled[:], in0=pooled[:], in1=gated_bias[:], op=ALU.add)
+        halves = [slice(0, P), slice(P, OUT)]
+        for cols in halves:
+            nc.vector.tensor_tensor(out=pooled[:, cols], in0=run_max[:, 0, cols], in1=run_max[:, 1, cols], op=ALU.max)
+        for cols in halves:
+            nc.vector.tensor_tensor(out=pooled[:, cols], in0=pooled[:, cols], in1=gated_bias[:, cols], op=ALU.add)
         nc.sync.dma_start(out=out_1, in_=pooled[:])

from contextlib import ExitStack

import concourse.mybir as mybir
from concourse.masks import make_identity

BF16 = mybir.dt.bfloat16
F32 = mybir.dt.float32
U32 = mybir.dt.uint32
U8 = mybir.dt.uint8
FP8X4 = mybir.dt.float8_e4m3fn_x4
ACT = mybir.ActivationFunctionType
ALU = mybir.AluOpType

P = 128
SLICES = 64
FEATURES = 1024
OUT = 256
EPS = 1e-5
CHUNKS = FEATURES // P
PACK = 4
PASSES = FEATURES // (P * PACK)
GROUP = 2
JOBS = 1 + SLICES // GROUP
HALVES = OUT // P
PAIR = 2
SCALAR_ROWS = 32
RUN = 8

FLOPS = 2 * (SLICES + 1) * P * FEATURES * OUT


def tile_cgblock_pb_t_kernel(
    tc, s_z2, c_z2, s_g2, s_be2, s_w3, s_b3, c_g2, c_be2, c_w3, c_b3, out_0, out_1
):
    nc = tc.nc
    with ExitStack() as stack:
        stack.enter_context(tc.manual_schedule())
        const = stack.enter_context(tc.tile_pool(name="const", bufs=1))
        small = stack.enter_context(tc.tile_pool(name="small", bufs=4))
        work = stack.enter_context(tc.tile_pool(name="work", bufs=3))
        results = stack.enter_context(tc.tile_pool(name="results", bufs=6))
        psum_x = stack.enter_context(tc.psum_pool(name="psum_x", bufs=6))
        psum_sum = stack.enter_context(tc.psum_pool(name="psum_sum", bufs=1))
        psum_acc = stack.enter_context(tc.psum_pool(name="psum_acc", bufs=1))

        blank = const.tile([P, OUT], BF16)
        nc.vector.memset(blank[:], 0.0)
        vec_rows = const.tile([P, P], BF16)
        nc.vector.memset(vec_rows[:], 0.0)
        bias_rows = const.tile([P, 2, OUT], BF16)
        nc.vector.memset(bias_rows[:], 0.0)
        for r, vec in enumerate((s_g2, s_be2, c_g2, c_be2)):
            nc.scalar.dma_start(
                out=vec_rows[r * CHUNKS : (r + 1) * CHUNKS, :],
                in_=vec.rearrange("(c p) -> c p", p=P),
            )
        for r, vec in enumerate((c_b3, s_b3)):
            nc.scalar.dma_start(out=bias_rows[0:1, r, :], in_=vec.unsqueeze(0))
        c_w_raw = const.tile([P, HALVES, FEATURES], BF16)
        c_x = const.tile([P, FEATURES], BF16)
        s_w_raw = const.tile([P, HALVES, FEATURES], BF16)
        x_tiles = [const.tile([P, GROUP, FEATURES], BF16, name="x_tile%d" % r) for r in range(SLICES // GROUP)]

        def load_weight(raw, w, h):
            nc.sync.dma_start(out=raw[:, h, :], in_=w[h * P : (h + 1) * P, :])

        def load_slices(r):
            nc.sync.dma_start(out=x_tiles[r][:], in_=s_z2[:, r * GROUP : (r + 1) * GROUP, :])

        load_weight(c_w_raw, c_w3, 0)
        nc.sync.dma_start(out=c_x[:], in_=c_z2)
        load_weight(c_w_raw, c_w3, 1)
        load_slices(0)
        for h in range(HALVES):
            load_weight(s_w_raw, s_w3, h)
        for r in range(1, SLICES // GROUP):
            load_slices(r)

        ident = const.tile([P, P], BF16)
        make_identity(nc, ident[:])
        ones = const.tile([P, P], BF16)
        nc.vector.memset(ones[:], 1.0)
        eps = const.tile([P, 1], F32)
        nc.vector.memset(eps[:], EPS)
        first_call = const.tile([P, 1], F32)
        nc.scalar.activation(out=first_call[:], in_=eps[:], func=ACT.Sqrt)

        def raise_clock(passes, bank):
            for r in range(passes):
                nc.tensor.matmul(out=bank[:, OUT : 2 * OUT], lhsT=blank[:, 0:P], rhs=blank[:], start=True, stop=True)

        def new_weight(raw, label):
            grouped = const.tile([P, PASSES, OUT, PACK], BF16, name="%s_grouped" % label, align_bytes=64)
            codes = const.tile([P, PASSES, OUT], U32, name="%s_codes" % label, align_bytes=64)
            scales = const.tile([P, PASSES, OUT], U8, name="%s_scales" % label, align_bytes=64)
            return {"raw": raw, "grouped": grouped, "codes": codes, "scales": scales, "banks": {}}

        def transpose_weight(weight, h):
            w_t = psum_x.tile([P, CHUNKS, P], BF16, tag="xt")
            for c in range(CHUNKS):
                nc.tensor.transpose(w_t[:, c, :], weight["raw"][:, h, c * P : (c + 1) * P], ident[:])
            weight["banks"][h] = w_t

        def regroup_weight(weight, h):
            for g in range(PASSES):
                nc.vector.tensor_copy(
                    out=weight["grouped"][:, g, h * P : (h + 1) * P, :],
                    in_=weight["banks"][h][:, g * PACK : (g + 1) * PACK, :].rearrange("p t n -> p n t"),
                )

        def quantise_weight(weight):
            nc.vector.quantize_mx(
                out=weight["codes"][:].rearrange("p g n -> p (g n)").bitcast(FP8X4),
                scales=weight["scales"][:].rearrange("p g n -> p (g n)"),
                in_=weight["grouped"][:].rearrange("p g n t -> p (g n t)"),
            )

        c_w = new_weight(c_w_raw, "c_w")
        s_w = new_weight(s_w_raw, "s_w")

        params = const.tile([P, 4, CHUNKS], F32)
        biases = const.tile([P, 2, OUT], F32)
        c_bias, s_bias = biases[:, 0, :], biases[:, 1, :]
        jobs = [{"x": [c_x[:]], "gain": params[:, 2, :], "shift": params[:, 3, :]}]
        for first in range(0, SLICES, GROUP):
            jobs.append(
                {
                    "x": [x_tiles[first // GROUP][:, s, :] for s in range(GROUP)],
                    "gain": params[:, 0, :],
                    "shift": params[:, 1, :],
                    "first": first,
                }
            )
        gate = const.tile([P, OUT], F32)
        gated_bias = const.tile([P, OUT], F32)
        run_max = const.tile([P, PAIR, OUT], F32)
        pairs = [{} for m in range(JOBS)]

        def live(j):
            return 0 <= j < JOBS

        def over_slices(vec, n):
            return vec.unsqueeze(1).to_broadcast([P, n, CHUNKS])

        def transpose_and_sum(j):
            if not live(j):
                return
            job = jobs[j]
            job["banks"] = []
            for x in job["x"]:
                x_t = psum_x.tile([P, CHUNKS, P], BF16, tag="xt")
                job["banks"].append(x_t)
            for g in range(PASSES):
                for x, x_t in zip(job["x"], job["banks"]):
                    for c in range(g * PACK, (g + 1) * PACK):
                        nc.tensor.transpose(x_t[:, c, :], x[:, c * P : (c + 1) * P], ident[:])
            sums_bank = psum_sum.tile([P, 2 * OUT], F32, tag="sums")
            sums = sums_bank[:, 0 : GROUP * CHUNKS].rearrange("p (s c) -> p s c", c=CHUNKS)
            job["sums_bank"] = sums_bank
            for s, x in enumerate(job["x"]):
                for c in range(CHUNKS):
                    nc.tensor.matmul(
                        out=sums[:, s, c : c + 1],
                        lhsT=x[:, c * P : (c + 1) * P],
                        rhs=ones[:, 0:1],
                        start=True,
                        stop=True,
                    )
            job["sums"] = sums

        def mean(j):
            if not live(j):
                return
            job = jobs[j]
            n = len(job["x"])
            neg_mean = small.tile([P, GROUP, CHUNKS], F32)
            nc.scalar.mul(out=neg_mean[:, :n, :], in_=job["sums"][:, :n, :], mul=-1.0 / P)
            job["neg_mean"] = neg_mean

        def deviations(j):
            if not live(j):
                return
            job = jobs[j]
            n = len(job["x"])
            dev2 = small.tile([P, GROUP, CHUNKS], F32)
            for s in range(n):
                for c in range(CHUNKS):
                    squares = work.tile([P, P], BF16)
                    nc.scalar.activation(
                        out=squares[:],
                        in_=job["banks"][s][:, c, :],
                        func=ACT.Square,
                        bias=job["neg_mean"][:, s, c : c + 1],
                        scale=1.0,
                        accum_out=dev2[:, s, c : c + 1],
                    )
            std = small.tile([P, GROUP, CHUNKS], F32)
            nc.scalar.activation(
                out=std[:, :n, :], in_=dev2[:, :n, :], func=ACT.Sqrt, bias=eps[:], scale=1.0 / P
            )
            job["std"] = std

        def inverse_std(j):
            if not live(j):
                return
            job = jobs[j]
            n = len(job["x"])
            a = small.tile([P, GROUP, CHUNKS], F32)
            nc.vector.reciprocal(out=a[:, :n, :], in_=job["std"][:, :n, :])
            job["a"] = a

        def scale(j):
            if not live(j):
                return
            job = jobs[j]
            n = len(job["x"])
            a = job["a"]
            nc.vector.tensor_tensor(out=a[:, :n, :], in0=a[:, :n, :], in1=over_slices(job["gain"], n), op=ALU.mult)

        def mean_times_scale(j):
            if not live(j):
                return
            job = jobs[j]
            n = len(job["x"])
            b = small.tile([P, GROUP, CHUNKS], F32)
            nc.vector.tensor_tensor(out=b[:, :n, :], in0=job["neg_mean"][:, :n, :], in1=job["a"][:, :n, :], op=ALU.mult)
            job["b"] = b

        def shift(j):
            if not live(j):
                return
            job = jobs[j]
            n = len(job["x"])
            b = job["b"]
            nc.vector.tensor_tensor(out=b[:, :n, :], in0=b[:, :n, :], in1=over_slices(job["shift"], n), op=ALU.add)

        def normalise(j):
            if not live(j):
                return
            job = jobs[j]
            planes = work.tile([P, GROUP, CHUNKS, P], BF16)
            for s in range(len(job["x"])):
                for c in range(CHUNKS):
                    out, x = planes[:, s, c, :], job["banks"][s][:, c, :]
                    a, b = job["a"][:, s, c : c + 1], job["b"][:, s, c : c + 1]
                    if j == JOBS - 1 and s == 1:
                        nc.scalar.activation(out=out, in_=x, func=ACT.Identity, bias=b, scale=a)
                    else:
                        nc.vector.tensor_scalar(out=out, in0=x, scalar1=a, scalar2=b, op0=ALU.mult, op1=ALU.add)
            job["planes"] = planes

        def regroup_views(job, s, g, rows):
            dst = job["grouped"][:, s, g, rows, :].rearrange("p (q i) t -> p q t i", i=RUN)
            src = job["planes"][:, s, g * PACK : (g + 1) * PACK, rows].rearrange("p t (q i) -> p q t i", i=RUN)
            return dst, src

        def blocks(job):
            return [(s, g) for s in range(len(job["x"])) for g in range(PASSES)]

        def scalar_rows(j):
            return 0 if j == JOBS - 1 else SCALAR_ROWS

        def regroup_on_vector(j, which):
            if not live(j):
                return
            job = jobs[j]
            if "grouped" not in job:
                job["grouped"] = work.tile([P, GROUP, PASSES, P, PACK], BF16, align_bytes=64, name="grouped")
            shared = blocks(job)[-2]
            for s, g in blocks(job)[:-1][which]:
                dst, src = regroup_views(job, s, g, slice(0, P - scalar_rows(j) if (s, g) == shared else P))
                nc.vector.tensor_scalar_max(out=dst, in0=src, scalar1=0.0)

        def regroup_on_scalar(j):
            if not live(j):
                return
            job = jobs[j]
            shared, own = blocks(job)[-2:]
            for (s, g), rows in ((shared, slice(P - scalar_rows(j), P)), (own, slice(0, P))):
                if rows.start < rows.stop:
                    dst, src = regroup_views(job, s, g, rows)
                    nc.scalar.activation(out=dst, in_=src, func=ACT.Relu)

        def quantise(j):
            if not live(j):
                return
            job = jobs[j]
            n = len(job["x"])
            codes = work.tile([P, GROUP, PASSES, P], U32, align_bytes=64)
            scales = work.tile([P, GROUP, PASSES, P], U8, align_bytes=64)
            nc.vector.quantize_mx(
                out=codes[:, :n, :, :].rearrange("p s g m -> p (s g m)").bitcast(FP8X4),
                scales=scales[:, :n, :, :].rearrange("p s g m -> p (s g m)"),
                in_=job["grouped"][:, :n, :, :, :].rearrange("p s g m t -> p (s g m t)"),
            )
            job["codes"] = codes
            job["scales"] = scales

        def project(j):
            if not live(j):
                return
            job = jobs[j]
            weight = c_w if j == 0 else s_w
            w_codes, w_scales = weight["codes"], weight["scales"]
            if j == JOBS - 1:
                acc = psum_x.tile([P, GROUP, OUT], F32, tag="xt")
            else:
                acc = psum_acc.tile([P, GROUP, OUT], F32, tag="acc")
            for s in range(len(job["x"])):
                for g in range(PASSES):
                    nc.tensor.matmul_mx(
                        out=acc[:, s, :],
                        lhsT=job["codes"][:, s, g, :].bitcast(FP8X4),
                        lhsT_scale=job["scales"][:, s, g, :],
                        rhs=w_codes[:, g, :].bitcast(FP8X4),
                        rhs_scale=w_scales[:, g, :],
                        start=(g == 0),
                        stop=(g == PASSES - 1),
                    )
            job["acc"] = acc

        def apply_gate(j, s):
            if not live(j):
                return
            job = jobs[j]
            if j == 0:
                if s == 0:
                    nc.vector.tensor_tensor(out=gate[:], in0=job["acc"][:, 0, :], in1=c_bias, op=ALU.add)
                else:
                    nc.vector.tensor_tensor(out=gated_bias[:], in0=gate[:], in1=s_bias, op=ALU.mult)
                return
            m, place = (j - 1, 1) if s == 0 else (j, 0)
            if s == 1 or j == 1:
                gated = work.tile([P, PAIR, OUT], F32)
                pairs[m]["gated"] = gated
            nc.vector.tensor_tensor(
                out=pairs[m]["gated"][:, place, :], in0=job["acc"][:, s, :], in1=gate[:], op=ALU.mult
            )

        def places(m):
            return slice(1 if m == 0 else 0, 1 if m == JOBS - 1 else PAIR)

        def add_bias_and_store(m, engine):
            if not 0 <= m < JOBS:
                return
            held = places(m)
            result = results.tile([P, PAIR, OUT], F32)
            bias = gated_bias[:].unsqueeze(1).to_broadcast([P, held.stop - held.start, OUT])
            engine.tensor_tensor(out=result[:, held, :], in0=pairs[m]["gated"][:, held, :], in1=bias, op=ALU.add)
            first = PAIR * m - 1
            nc.sync.dma_start(out=out_0[:, first + held.start : first + held.stop, :], in_=result[:, held, :])

        def pool(m):
            if not 0 <= m < JOBS:
                return
            gated = pairs[m]["gated"]
            if m == 0:
                nc.vector.tensor_copy(out=run_max[:], in_=gated[:, 1, :].unsqueeze(1).to_broadcast([P, PAIR, OUT]))
            else:
                held = places(m)
                nc.vector.tensor_tensor(out=run_max[:, held, :], in0=run_max[:, held, :], in1=gated[:, held, :], op=ALU.max)

        every, early, late = slice(None), slice(0, -1), slice(-1, None)

        def short_steps(j):
            inverse_std(j)
            scale(j)
            mean_times_scale(j)
            shift(j)

        head_bank = psum_sum.tile([P, 2 * OUT], F32, tag="sums")
        raise_clock(12, head_bank)
        transpose_weight(c_w, 0)
        regroup_weight(c_w, 0)
        transpose_and_sum(0)
        mean(0)
        deviations(0)
        transpose_weight(c_w, 1)
        regroup_weight(c_w, 1)
        raise_clock(4, jobs[0]["sums_bank"])

        bias_bank = psum_acc.tile([P, 2 * OUT], F32, tag="acc")
        nc.tensor.matmul(
            out=bias_bank[:], lhsT=ones[:], rhs=bias_rows[:].rearrange("p r n -> p (r n)"), start=True, stop=True
        )
        vec_t = psum_x.tile([P, CHUNKS, P], BF16, tag="xt")
        nc.tensor.transpose(vec_t[:, 0, :], vec_rows[:], ident[:])
        nc.vector.tensor_copy(
            out=params[:].rearrange("p r c -> p (r c)"), in_=vec_t[:, 0, 0 : 4 * CHUNKS]
        )

        transpose_and_sum(1)
        mean(1)
        quantise_weight(c_w)
        short_steps(0)
        normalise(0)
        regroup_on_vector(0, every)
        for h in range(HALVES):
            transpose_weight(s_w, h)
        regroup_weight(s_w, 0)
        deviations(1)
        nc.scalar.copy(out=biases[:].rearrange("p r n -> p (r n)"), in_=bias_bank[:])
        regroup_weight(s_w, 1)
        quantise_weight(s_w)
        transpose_and_sum(2)
        mean(2)
        regroup_on_scalar(0)
        short_steps(1)
        deviations(2)
        normalise(1)
        regroup_on_vector(1, every)
        quantise(0)
        transpose_and_sum(3)
        mean(3)
        regroup_on_scalar(1)

        for k in range(2, JOBS):
            project(k - 2)
            inverse_std(k)
            pool(k - 4)
            scale(k)
            quantise(k - 1)
            mean_times_scale(k)
            apply_gate(k - 2, 0)
            shift(k)
            apply_gate(k - 2, 1)
            add_bias_and_store(k - 3, nc.gpsimd)
            deviations(k + 1)
            normalise(k)
            regroup_on_vector(k, early if k == JOBS - 1 else every)
            transpose_and_sum(k + 2)
            mean(k + 2)
            regroup_on_scalar(k)

        last = JOBS - 1
        project(last - 1)
        pool(last - 3)
        regroup_on_vector(last, late)
        quantise(last)
        project(last)
        apply_gate(last - 1, 0)
        apply_gate(last - 1, 1)
        add_bias_and_store(last - 2, nc.gpsimd)
        apply_gate(last, 0)
        apply_gate(last, 1)
        pool(last - 2)
        add_bias_and_store(last - 1, nc.vector)
        pool(last - 1)
        add_bias_and_store(last, nc.vector)
        pool(last)
        pooled = const.tile([P, OUT], F32)
        halves = [slice(0, P), slice(P, OUT)]
        for cols in halves:
            nc.vector.tensor_tensor(out=pooled[:, cols], in0=run_max[:, 0, cols], in1=run_max[:, 1, cols], op=ALU.max)
        for cols in halves:
            nc.vector.tensor_tensor(out=pooled[:, cols], in0=pooled[:, cols], in1=gated_bias[:, cols], op=ALU.add)
        nc.sync.dma_start(out=out_1, in_=pooled[:])
